import numpy as np
import ml_dtypes


def mxq(x, axis, fmt="e4m3"):
    dtype, down = {"e4m3": (ml_dtypes.float8_e4m3fn, 7), "e5m2": (ml_dtypes.float8_e5m2, 14)}[fmt]
    v = np.moveaxis(np.asarray(x, np.float32).astype(ml_dtypes.bfloat16).astype(np.float64), axis, -1)
    blocks = v.reshape(v.shape[:-1] + (-1, 32))
    amax = np.abs(blocks).max(-1, keepdims=True)
    byte = np.maximum(np.where(amax > 0, np.frexp(amax)[1] - 1 + 127, 0) - down, 1)
    scale = np.exp2(byte - 127.0)
    codes = (blocks / scale).astype(np.float32).astype(dtype).astype(np.float64)
    return np.moveaxis((codes * scale).reshape(v.shape), -1, axis)


WIDE = False


def mx_kscale(k):
    if not WIDE:
        return np.ones(k)
    levels = np.array([10, -10, 5, -5, 0])
    if k % 512:
        return np.exp2(np.random.permutation(np.resize(levels, k // 32))).repeat(32)
    a = np.empty((k // 512, 16))
    for p in range(k // 512):
        a[p, :8] = np.random.permutation(np.resize(levels, 8))
        for g in range(8):
            far = levels[np.abs(levels - a[p, g]) >= 10]
            a[p, g + 8] = far[np.random.randint(len(far))]
    return np.exp2(a.ravel()).repeat(32)


BF16 = ml_dtypes.bfloat16


def bf(x):
    return np.asarray(x, np.float32).astype(BF16)


def f64(x):
    return np.asarray(x).astype(np.float64)


N, S, D, H, O = 4, 1024, 1024, 512, 1024


def elu(v):
    return np.where(v > 0.0, v, np.exp(np.minimum(v, 0.0)) - 1.0)


def setup_inputs():
    s = mx_kscale(D)
    return {"x": bf(np.random.standard_normal((N, S, D)) * s),
            "Wk": bf(np.random.standard_normal((D, H)) / np.sqrt(D) / s[:, None]),
            "bk": bf(np.random.standard_normal(H) * 0.1),
            "Wv": bf(np.random.standard_normal((D, H)) / np.sqrt(D) / s[:, None]),
            "bv": bf(np.random.standard_normal(H) * 0.1)}


def reference(x, Wk, bk, Wv, bv):
    xq = mxq(f64(x), 2, "e4m3")
    keyp = (xq @ mxq(f64(Wk), 0, "e4m3")) + f64(bk)
    value = (xq @ mxq(f64(Wv), 0, "e4m3")) + f64(bv)
    K = elu(keyp) + 1.0
    KV = np.sum(K * value, axis=1)
    Ksum = np.sum(K, axis=1)
    return KV, Ksum

@@ -1,0 +1,247 @@
+from contextlib import ExitStack
+
+import concourse.mybir as mybir
+from concourse.masks import make_identity
+
+F32 = mybir.dt.float32
+BF16 = mybir.dt.bfloat16
+U32 = mybir.dt.uint32
+U8 = mybir.dt.uint8
+FP8X4 = mybir.dt.float8_e4m3fn_x4
+ACT = mybir.ActivationFunctionType
+ALU = mybir.AluOpType
+AXIS = mybir.AxisListType
+
+P = 128
+PACK = 4
+BATCH, SEQ, D, H = 4, 1024, 1024, 512
+PASSES = D // (P * PACK)
+CHUNK = 512
+CHUNKS = BATCH * SEQ // CHUNK
+CHUNKS_PER_BATCH = SEQ // CHUNK
+ROWS = CHUNK // P
+WORDS = D // 2
+H_TILES = H // P
+UNITS = CHUNKS * PASSES
+STEP_TILES = 2
+STEPS = CHUNKS * H_TILES // STEP_TILES
+
+FLOPS = 2 * BATCH * SEQ * D * (2 * H)
+
+
+def tile_linearattention_pa_t_kernel(tc, x, Wk, bk, Wv, bv, out_0, out_1):
+    nc = tc.nc
+    with ExitStack() as ctx:
+        ctx.enter_context(tc.manual_schedule())
+        const = ctx.enter_context(tc.tile_pool(name="const", bufs=1))
+        x_pool = ctx.enter_context(tc.tile_pool(name="x", bufs=1))
+        w_pool = ctx.enter_context(tc.tile_pool(name="w", bufs=1))
+        xq_pool = ctx.enter_context(tc.tile_pool(name="xq", bufs=2))
+        work = ctx.enter_context(tc.tile_pool(name="work", bufs=4))
+        psum_t = ctx.enter_context(tc.psum_pool(name="psum_t", bufs=2))
+        psum_k = ctx.enter_context(tc.psum_pool(name="psum_k", bufs=4))
+        psum_v = ctx.enter_context(tc.psum_pool(name="psum_v", bufs=2))
+
+        x_chunks = x.flatten_outer_dims().rearrange("(c p r) d -> c p (r d)", p=P, r=ROWS)
+        x_tiles = [x_pool.tile([P, ROWS * D], BF16, name="x%d" % c) for c in range(CHUNKS)]
+
+        def load_weight(w, label):
+            raw = w_pool.tile([P, PASSES * PACK, H], BF16, name="raw_" + label)
+            for g in range(PASSES):
+                nc.sync.dma_start(
+                    out=raw[:, g * PACK : (g + 1) * PACK, :].rearrange("p t h -> p (t h)"),
+                    in_=w[g * P * PACK : (g + 1) * P * PACK, :].rearrange("(p t) h -> p (t h)", t=PACK),
+                )
+            return raw
+
+        bias_rows = const.tile([P, P], BF16)
+        nc.vector.memset(bias_rows[:], 0.0)
+        nc.sync.dma_start(out=x_tiles[0][:], in_=x_chunks[0])
+        nc.sync.dma_start(out=bias_rows[0:H_TILES, :], in_=bk.rearrange("(j h) -> j h", h=P))
+        nc.sync.dma_start(out=bias_rows[H_TILES : 2 * H_TILES, :], in_=bv.rearrange("(j h) -> j h", h=P))
+        raw_k = load_weight(Wk, "k")
+        nc.sync.dma_start(out=x_tiles[1][:], in_=x_chunks[1])
+        raw_v = load_weight(Wv, "v")
+        for c in range(2, CHUNKS):
+            nc.sync.dma_start(out=x_tiles[c][:], in_=x_chunks[c])
+
+        ident = const.tile([P, P], F32)
+        make_identity(nc, ident[:])
+
+        warm = const.tile([P, 2], F32)
+        nc.vector.memset(warm[:], 0.0)
+        nc.scalar.activation(out=warm[:, 1:2], in_=warm[:, 0:1], func=ACT.Exp)
+        totals = const.tile([P, P], F32)
+        nc.vector.memset(totals[:], 0.0)
+        bias_rows_f32 = const.tile([P, P], F32)
+        nc.vector.tensor_copy(out=bias_rows_f32[:], in_=bias_rows[:])
+        bias = const.tile([P, 2 * H_TILES], F32)
+        bk_plus_1 = const.tile([P, H_TILES], F32)
+
+        def spread_biases():
+            bias_bank = psum_t.tile([P, P], F32, tag="t")
+            nc.tensor.transpose(bias_bank[:], bias_rows_f32[:], ident[:])
+            nc.vector.tensor_copy(out=bias[:], in_=bias_bank[:, 0 : 2 * H_TILES])
+            nc.vector.tensor_scalar_add(out=bk_plus_1[:], in0=bias[:, 0:H_TILES], scalar1=1.0)
+
+        parts = const.tile([P, 2, BATCH * H_TILES * CHUNKS_PER_BATCH], F32)
+
+        def regroup_weight(raw, label):
+            grouped = w_pool.tile([P, PASSES * H * PACK], BF16, name="grouped_" + label, align_bytes=64)
+            for g in range(PASSES):
+                nc.vector.tensor_copy(
+                    out=grouped[:, g * H * PACK : (g + 1) * H * PACK].rearrange(
+                        "p (c i t) -> p c t i", i=4, t=PACK
+                    ),
+                    in_=raw[:, g * PACK : (g + 1) * PACK, :].rearrange("p t (c i) -> p c t i", i=4),
+                )
+            return grouped
+
+        def quantise_weight(grouped, label):
+            codes = w_pool.tile([P, PASSES * H], U32, name="codes_" + label, align_bytes=64)
+            scales = w_pool.tile([P, PASSES * H], U8, name="scales_" + label, align_bytes=64)
+            nc.vector.quantize_mx(out=codes[:].bitcast(FP8X4), scales=scales[:], in_=grouped[:])
+            return codes, scales
+
+        grouped_x = {}
+        x_codes = {}
+
+        def transpose_unit(unit):
+            c, g = divmod(unit, PASSES)
+            if g == 0:
+                grouped_x[c] = xq_pool.tile([P, PASSES * CHUNK * PACK], BF16, name="grouped_x", align_bytes=64)
+            words_in = x_tiles[c][:].bitcast(F32)
+            words_out = grouped_x[c][:].bitcast(F32)
+            for half in range(2):
+                bank = psum_t.tile([P, 2, 2 * P], F32, tag="t")
+                for u in range(2):
+                    for r in range(2):
+                        row = (2 * half + r) * WORDS + 2 * P * g
+                        nc.tensor.transpose(
+                            bank[:, u, r * P : (r + 1) * P], words_in[:, row + u : row + 2 * P : 2], ident[:]
+                        )
+                start = 2 * (g * CHUNK + half * 2 * P)
+                nc.scalar.copy(
+                    out=words_out[:, start : start + 4 * P].rearrange("p (s u) -> p s u", u=2),
+                    in_=bank[:].rearrange("p u s -> p s u"),
+                )
+
+        def quantise_chunk(c):
+            codes = xq_pool.tile([P, PASSES * CHUNK], U32, name="codes_x", align_bytes=64)
+            scales = xq_pool.tile([P, PASSES * CHUNK], U8, name="scales_x", align_bytes=64)
+            nc.vector.quantize_mx(out=codes[:].bitcast(FP8X4), scales=scales[:], in_=grouped_x[c][:])
+            x_codes[c] = (codes, scales)
+
+        def product(bank, weight, c, j):
+            w_codes, w_scales = weight
+            codes, scales = x_codes[c]
+            for g in range(PASSES):
+                w_cols = slice(g * H + j * P, g * H + (j + 1) * P)
+                x_cols = slice(g * CHUNK, (g + 1) * CHUNK)
+                nc.tensor.matmul_mx(
+                    out=bank[:],
+                    lhsT=w_codes[:, w_cols].bitcast(FP8X4),
+                    lhsT_scale=w_scales[:, w_cols],
+                    rhs=codes[:, x_cols].bitcast(FP8X4),
+                    rhs_scale=scales[:, x_cols],
+                    start=(g == 0),
+                    stop=(g == PASSES - 1),
+                )
+
+        def blocks_of(step):
+            c, part = divmod(step, H_TILES // STEP_TILES)
+            return c, range(part * STEP_TILES, (part + 1) * STEP_TILES)
+
+        def part_column(c, j):
+            n, chunk_of_batch = divmod(c, CHUNKS_PER_BATCH)
+            return (n * H_TILES + j) * CHUNKS_PER_BATCH + chunk_of_batch
+
+        key_banks = {}
+        small_exps = {}
+
+        def key_stage(step):
+            c, blocks = blocks_of(step)
+            for j in blocks:
+                key_banks[(c, j)] = psum_k.tile([P, CHUNK], F32, tag="k", name="key_bank")
+                product(key_banks[(c, j)], weight_k, c, j)
+            for j in blocks:
+                small_exps[(c, j)] = work.tile([P, CHUNK], F32, tag="small_exp", name="small_exp")
+                nc.scalar.activation(
+                    out=small_exps[(c, j)][:], in_=key_banks[(c, j)][:], func=ACT.Exp, bias=bias[:, j : j + 1]
+                )
+                nc.gpsimd.tensor_scalar(
+                    out=small_exps[(c, j)][:],
+                    in0=small_exps[(c, j)][:],
+                    scalar1=1.0,
+                    scalar2=0.0,
+                    op0=ALU.min,
+                    op1=ALU.max,
+                )
+
+        def value_stage(step):
+            c, blocks = blocks_of(step)
+            value_banks = {}
+            features = {}
+            for j in blocks:
+                value_banks[j] = psum_v.tile([P, CHUNK], F32, tag="v", name="value_bank")
+                product(value_banks[j], weight_v, c, j)
+            for j in blocks:
+                column = part_column(c, j)
+                features[j] = work.tile([P, CHUNK], F32, tag="feature", name="feature")
+                nc.vector.scalar_tensor_tensor(
+                    out=features[j][:],
+                    in0=key_banks[(c, j)][:],
+                    scalar=bk_plus_1[:, j : j + 1],
+                    in1=small_exps[(c, j)][:],
+                    op0=ALU.add,
+                    op1=ALU.max,
+                    accum_out=parts[:, 1, column : column + 1],
+                )
+            for j in blocks:
+                column = part_column(c, j)
+                weighted = work.tile([P, CHUNK], F32, tag="weighted")
+                nc.vector.scalar_tensor_tensor(
+                    out=weighted[:],
+                    in0=value_banks[j][:],
+                    scalar=bias[:, H_TILES + j : H_TILES + j + 1],
+                    in1=features[j][:],
+                    op0=ALU.add,
+                    op1=ALU.mult,
+                    accum_out=parts[:, 0, column : column + 1],
+                )
+
+        transpose_unit(0)
+        transpose_unit(1)
+        grouped_k = regroup_weight(raw_k, "k")
+        spread_biases()
+        weight_k = quantise_weight(grouped_k, "k")
+        quantise_chunk(0)
+        transpose_unit(2)
+        transpose_unit(3)
+        key_stage(0)
+        grouped_v = regroup_weight(raw_v, "v")
+        weight_v = quantise_weight(grouped_v, "v")
+        steps_per_chunk = H_TILES // STEP_TILES
+        for step in range(STEPS):
+            next_chunk = step // steps_per_chunk + 1
+            if step % steps_per_chunk == 0 and next_chunk < CHUNKS:
+                quantise_chunk(next_chunk)
+            if step + 4 < UNITS:
+                transpose_unit(step + 4)
+            if step + 1 < STEPS:
+                key_stage(step + 1)
+            value_stage(step)
+
+        results = BATCH * H_TILES
+        nc.vector.tensor_reduce(
+            out=totals[:, 0 : 2 * results],
+            in_=parts[:].rearrange("p w (r k) -> p (w r) k", k=CHUNKS_PER_BATCH),
+            axis=AXIS.X,
+            op=ALU.add,
+        )
+        totals_bank = psum_t.tile([P, P], F32, tag="t")
+        nc.tensor.transpose(totals_bank[:], totals[:], ident[:])
+        rows = const.tile([P, P], F32)
+        nc.vector.tensor_copy(out=rows[:], in_=totals_bank[:])
+        nc.sync.dma_start(out=out_0.rearrange("n (j h) -> (n j) h", h=P), in_=rows[0:results, :])
+        nc.sync.dma_start(out=out_1.rearrange("n (j h) -> (n j) h", h=P), in_=rows[results : 2 * results, :])

@@ -25,6 +25,7 @@ H_TILES = H // P
 UNITS = CHUNKS * PASSES
 STEP_TILES = 2
 STEPS = CHUNKS * H_TILES // STEP_TILES
+SUM_BLOCK = 0
 
 FLOPS = 2 * BATCH * SEQ * D * (2 * H)
 
@@ -77,14 +78,17 @@ def tile_linearattention_pa_t_kernel(tc, x, Wk, bk, Wv, bv, out_0, out_1):
         nc.vector.tensor_copy(out=bias_rows_f32[:], in_=bias_rows[:])
         bias = const.tile([P, 2 * H_TILES], F32)
         bk_plus_1 = const.tile([P, H_TILES], F32)
+        minus_bk = const.tile([P, H_TILES], F32)
 
         def spread_biases():
             bias_bank = psum_t.tile([P, P], F32, tag="t")
             nc.tensor.transpose(bias_bank[:], bias_rows_f32[:], ident[:])
             nc.vector.tensor_copy(out=bias[:], in_=bias_bank[:, 0 : 2 * H_TILES])
             nc.vector.tensor_scalar_add(out=bk_plus_1[:], in0=bias[:, 0:H_TILES], scalar1=1.0)
+            nc.vector.tensor_scalar_mul(out=minus_bk[:], in0=bias[:, 0:H_TILES], scalar1=-1.0)
 
-        parts = const.tile([P, 2, BATCH * H_TILES * CHUNKS_PER_BATCH], F32)
+        parts = const.tile([P, 2, 2 * BATCH * H_TILES * CHUNKS_PER_BATCH], F32)
+        nc.vector.memset(parts[:], 0.0)
 
         def regroup_weight(raw, label):
             grouped = w_pool.tile([P, PASSES * H * PACK], BF16, name="grouped_" + label, align_bytes=64)
@@ -154,10 +158,37 @@ def tile_linearattention_pa_t_kernel(tc, x, Wk, bk, Wv, bv, out_0, out_1):
 
         def part_column(c, j):
             n, chunk_of_batch = divmod(c, CHUNKS_PER_BATCH)
-            return (n * H_TILES + j) * CHUNKS_PER_BATCH + chunk_of_batch
+            return 2 * ((n * H_TILES + j) * CHUNKS_PER_BATCH + chunk_of_batch)
 
         key_banks = {}
         small_exps = {}
+        features = {}
+
+        def sum_feature(c, j):
+            bank = key_banks[(c, j)]
+            column = part_column(c, j)
+            depth = work.tile([P, CHUNK], F32, tag="depth", name="depth")
+            nc.scalar.activation(
+                out=depth[:], in_=bank[:], func=ACT.Relu, bias=minus_bk[:, j : j + 1], scale=-1.0
+            )
+            rise = work.tile([P, CHUNK], F32, tag="rise", name="rise")
+            nc.scalar.activation(
+                out=rise[:],
+                in_=bank[:],
+                func=ACT.Relu,
+                bias=bias[:, j : j + 1],
+                accum_out=parts[:, 1, column : column + 1],
+            )
+            decay = work.tile([P, CHUNK], F32, tag="decay", name="decay")
+            nc.scalar.activation(
+                out=decay[:],
+                in_=depth[:],
+                func=ACT.Exp,
+                scale=-1.0,
+                accum_out=parts[:, 1, column + 1 : column + 2],
+            )
+            features[(c, j)] = work.tile([P, CHUNK], F32, tag="feature", name="feature")
+            nc.gpsimd.tensor_tensor(out=features[(c, j)][:], in0=rise[:], in1=decay[:], op=ALU.add)
 
         def key_stage(step):
             c, blocks = blocks_of(step)
@@ -165,6 +196,9 @@ def tile_linearattention_pa_t_kernel(tc, x, Wk, bk, Wv, bv, out_0, out_1):
                 key_banks[(c, j)] = psum_k.tile([P, CHUNK], F32, tag="k", name="key_bank")
                 product(key_banks[(c, j)], weight_k, c, j)
             for j in blocks:
+                if j == SUM_BLOCK:
+                    sum_feature(c, j)
+                    continue
                 small_exps[(c, j)] = work.tile([P, CHUNK], F32, tag="small_exp", name="small_exp")
                 nc.scalar.activation(
                     out=small_exps[(c, j)][:], in_=key_banks[(c, j)][:], func=ACT.Exp, bias=bias[:, j : j + 1]
@@ -181,15 +215,16 @@ def tile_linearattention_pa_t_kernel(tc, x, Wk, bk, Wv, bv, out_0, out_1):
         def value_stage(step):
             c, blocks = blocks_of(step)
             value_banks = {}
-            features = {}
             for j in blocks:
                 value_banks[j] = psum_v.tile([P, CHUNK], F32, tag="v", name="value_bank")
                 product(value_banks[j], weight_v, c, j)
             for j in blocks:
+                if j == SUM_BLOCK:
+                    continue
                 column = part_column(c, j)
-                features[j] = work.tile([P, CHUNK], F32, tag="feature", name="feature")
+                features[(c, j)] = work.tile([P, CHUNK], F32, tag="feature", name="feature")
                 nc.vector.scalar_tensor_tensor(
-                    out=features[j][:],
+                    out=features[(c, j)][:],
                     in0=key_banks[(c, j)][:],
                     scalar=bk_plus_1[:, j : j + 1],
                     in1=small_exps[(c, j)][:],
@@ -204,7 +239,7 @@ def tile_linearattention_pa_t_kernel(tc, x, Wk, bk, Wv, bv, out_0, out_1):
                     out=weighted[:],
                     in0=value_banks[j][:],
                     scalar=bias[:, H_TILES + j : H_TILES + j + 1],
-                    in1=features[j][:],
+                    in1=features[(c, j)][:],
                     op0=ALU.add,
                     op1=ALU.mult,
                     accum_out=parts[:, 0, column : column + 1],
@@ -235,7 +270,7 @@ def tile_linearattention_pa_t_kernel(tc, x, Wk, bk, Wv, bv, out_0, out_1):
         results = BATCH * H_TILES
         nc.vector.tensor_reduce(
             out=totals[:, 0 : 2 * results],
-            in_=parts[:].rearrange("p w (r k) -> p (w r) k", k=CHUNKS_PER_BATCH),
+            in_=parts[:].rearrange("p w (r k) -> p (w r) k", k=2 * CHUNKS_PER_BATCH),
             axis=AXIS.X,
             op=ALU.add,
         )

@@ -23,9 +23,14 @@ ROWS = CHUNK // P
 WORDS = D // 2
 H_TILES = H // P
 UNITS = CHUNKS * PASSES
-STEP_TILES = 2
-STEPS = CHUNKS * H_TILES // STEP_TILES
-SUM_BLOCK = 0
+TILES = CHUNKS * H_TILES
+UNIT_TILES = H_TILES // PASSES
+
+FEATURE_AHEAD = 1
+KEY_AHEAD = 3
+QUANTISE_AHEAD = 5
+TRANSPOSE_AHEAD = 9
+SUM_BLOCK = 3
 
 FLOPS = 2 * BATCH * SEQ * D * (2 * H)
 
@@ -37,7 +42,7 @@ def tile_linearattention_pa_t_kernel(tc, x, Wk, bk, Wv, bv, out_0, out_1):
         const = ctx.enter_context(tc.tile_pool(name="const", bufs=1))
         x_pool = ctx.enter_context(tc.tile_pool(name="x", bufs=1))
         w_pool = ctx.enter_context(tc.tile_pool(name="w", bufs=1))
-        xq_pool = ctx.enter_context(tc.tile_pool(name="xq", bufs=2))
+        xq_pool = ctx.enter_context(tc.tile_pool(name="xq", bufs=3))
         work = ctx.enter_context(tc.tile_pool(name="work", bufs=4))
         psum_t = ctx.enter_context(tc.psum_pool(name="psum_t", bufs=2))
         psum_k = ctx.enter_context(tc.psum_pool(name="psum_k", bufs=4))
@@ -136,7 +141,8 @@ def tile_linearattention_pa_t_kernel(tc, x, Wk, bk, Wv, bv, out_0, out_1):
             nc.vector.quantize_mx(out=codes[:].bitcast(FP8X4), scales=scales[:], in_=grouped_x[c][:])
             x_codes[c] = (codes, scales)
 
-        def product(bank, weight, c, j):
+        def product(bank, weight, tile):
+            c, j = divmod(tile, H_TILES)
             w_codes, w_scales = weight
             codes, scales = x_codes[c]
             for g in range(PASSES):
@@ -152,11 +158,8 @@ def tile_linearattention_pa_t_kernel(tc, x, Wk, bk, Wv, bv, out_0, out_1):
                     stop=(g == PASSES - 1),
                 )
 
-        def blocks_of(step):
-            c, part = divmod(step, H_TILES // STEP_TILES)
-            return c, range(part * STEP_TILES, (part + 1) * STEP_TILES)
-
-        def part_column(c, j):
+        def part_column(tile):
+            c, j = divmod(tile, H_TILES)
             n, chunk_of_batch = divmod(c, CHUNKS_PER_BATCH)
             return 2 * ((n * H_TILES + j) * CHUNKS_PER_BATCH + chunk_of_batch)
 
@@ -164,17 +167,20 @@ def tile_linearattention_pa_t_kernel(tc, x, Wk, bk, Wv, bv, out_0, out_1):
         small_exps = {}
         features = {}
 
-        def sum_feature(c, j):
-            bank = key_banks[(c, j)]
-            column = part_column(c, j)
+        def on_scalar(tile):
+            return tile % H_TILES == SUM_BLOCK and tile >= H_TILES
+
+        def sum_feature(tile):
+            j = tile % H_TILES
+            column = part_column(tile)
             depth = work.tile([P, CHUNK], F32, tag="depth", name="depth")
             nc.scalar.activation(
-                out=depth[:], in_=bank[:], func=ACT.Relu, bias=minus_bk[:, j : j + 1], scale=-1.0
+                out=depth[:], in_=key_banks[tile][:], func=ACT.Relu, bias=minus_bk[:, j : j + 1], scale=-1.0
             )
             rise = work.tile([P, CHUNK], F32, tag="rise", name="rise")
             nc.scalar.activation(
                 out=rise[:],
-                in_=bank[:],
+                in_=key_banks[tile][:],
                 func=ACT.Relu,
                 bias=bias[:, j : j + 1],
                 accum_out=parts[:, 1, column : column + 1],
@@ -187,85 +193,86 @@ def tile_linearattention_pa_t_kernel(tc, x, Wk, bk, Wv, bv, out_0, out_1):
                 scale=-1.0,
                 accum_out=parts[:, 1, column + 1 : column + 2],
             )
-            features[(c, j)] = work.tile([P, CHUNK], F32, tag="feature", name="feature")
-            nc.gpsimd.tensor_tensor(out=features[(c, j)][:], in0=rise[:], in1=decay[:], op=ALU.add)
+            features[tile] = work.tile([P, CHUNK], F32, tag="feature", name="feature")
+            nc.gpsimd.tensor_tensor(out=features[tile][:], in0=rise[:], in1=decay[:], op=ALU.add)
 
-        def key_stage(step):
-            c, blocks = blocks_of(step)
-            for j in blocks:
-                key_banks[(c, j)] = psum_k.tile([P, CHUNK], F32, tag="k", name="key_bank")
-                product(key_banks[(c, j)], weight_k, c, j)
-            for j in blocks:
-                if j == SUM_BLOCK:
-                    sum_feature(c, j)
-                    continue
-                small_exps[(c, j)] = work.tile([P, CHUNK], F32, tag="small_exp", name="small_exp")
-                nc.scalar.activation(
-                    out=small_exps[(c, j)][:], in_=key_banks[(c, j)][:], func=ACT.Exp, bias=bias[:, j : j + 1]
-                )
-                nc.gpsimd.tensor_scalar(
-                    out=small_exps[(c, j)][:],
-                    in0=small_exps[(c, j)][:],
-                    scalar1=1.0,
-                    scalar2=0.0,
-                    op0=ALU.min,
-                    op1=ALU.max,
-                )
+        def key_stage(tile):
+            j = tile % H_TILES
+            key_banks[tile] = psum_k.tile([P, CHUNK], F32, tag="k", name="key_bank")
+            product(key_banks[tile], weight_k, tile)
+            if on_scalar(tile):
+                sum_feature(tile)
+                return
+            small_exps[tile] = work.tile([P, CHUNK], F32, tag="small_exp", name="small_exp")
+            nc.scalar.activation(
+                out=small_exps[tile][:], in_=key_banks[tile][:], func=ACT.Exp, bias=bias[:, j : j + 1]
+            )
+            nc.gpsimd.tensor_scalar(
+                out=small_exps[tile][:],
+                in0=small_exps[tile][:],
+                scalar1=1.0,
+                scalar2=0.0,
+                op0=ALU.min,
+                op1=ALU.max,
+            )
 
-        def value_stage(step):
-            c, blocks = blocks_of(step)
-            value_banks = {}
-            for j in blocks:
-                value_banks[j] = psum_v.tile([P, CHUNK], F32, tag="v", name="value_bank")
-                product(value_banks[j], weight_v, c, j)
-            for j in blocks:
-                if j == SUM_BLOCK:
-                    continue
-                column = part_column(c, j)
-                features[(c, j)] = work.tile([P, CHUNK], F32, tag="feature", name="feature")
-                nc.vector.scalar_tensor_tensor(
-                    out=features[(c, j)][:],
-                    in0=key_banks[(c, j)][:],
-                    scalar=bk_plus_1[:, j : j + 1],
-                    in1=small_exps[(c, j)][:],
-                    op0=ALU.add,
-                    op1=ALU.max,
-                    accum_out=parts[:, 1, column : column + 1],
-                )
-            for j in blocks:
-                column = part_column(c, j)
-                weighted = work.tile([P, CHUNK], F32, tag="weighted")
-                nc.vector.scalar_tensor_tensor(
-                    out=weighted[:],
-                    in0=value_banks[j][:],
-                    scalar=bias[:, H_TILES + j : H_TILES + j + 1],
-                    in1=features[(c, j)][:],
-                    op0=ALU.add,
-                    op1=ALU.mult,
-                    accum_out=parts[:, 0, column : column + 1],
-                )
+        def feature_stage(tile):
+            if on_scalar(tile):
+                return
+            j = tile % H_TILES
+            column = part_column(tile)
+            features[tile] = work.tile([P, CHUNK], F32, tag="feature", name="feature")
+            nc.vector.scalar_tensor_tensor(
+                out=features[tile][:],
+                in0=key_banks[tile][:],
+                scalar=bk_plus_1[:, j : j + 1],
+                in1=small_exps[tile][:],
+                op0=ALU.add,
+                op1=ALU.max,
+                accum_out=parts[:, 1, column : column + 1],
+            )
 
-        transpose_unit(0)
-        transpose_unit(1)
+        def weigh_stage(tile, bank):
+            j = tile % H_TILES
+            column = part_column(tile)
+            weighted = work.tile([P, CHUNK], F32, tag="weighted")
+            nc.vector.scalar_tensor_tensor(
+                out=weighted[:],
+                in0=bank[:],
+                scalar=bias[:, H_TILES + j : H_TILES + j + 1],
+                in1=features[tile][:],
+                op0=ALU.add,
+                op1=ALU.mult,
+                accum_out=parts[:, 0, column : column + 1],
+            )
+
+        for unit in range(PASSES):
+            transpose_unit(unit)
         grouped_k = regroup_weight(raw_k, "k")
         spread_biases()
         weight_k = quantise_weight(grouped_k, "k")
         quantise_chunk(0)
-        transpose_unit(2)
-        transpose_unit(3)
-        key_stage(0)
         grouped_v = regroup_weight(raw_v, "v")
-        weight_v = quantise_weight(grouped_v, "v")
-        steps_per_chunk = H_TILES // STEP_TILES
-        for step in range(STEPS):
-            next_chunk = step // steps_per_chunk + 1
-            if step % steps_per_chunk == 0 and next_chunk < CHUNKS:
-                quantise_chunk(next_chunk)
-            if step + 4 < UNITS:
-                transpose_unit(step + 4)
-            if step + 1 < STEPS:
-                key_stage(step + 1)
-            value_stage(step)
+        weight_v = None
+
+        for slot in range(-5, TILES):
+            if slot == -2:
+                weight_v = quantise_weight(grouped_v, "v")
+            chunk, rest = divmod(slot + QUANTISE_AHEAD, H_TILES)
+            if rest == 0 and 0 < chunk < CHUNKS:
+                quantise_chunk(chunk)
+            unit, rest = divmod(slot + TRANSPOSE_AHEAD, UNIT_TILES)
+            if rest == 0 and unit < UNITS:
+                transpose_unit(unit)
+            if 0 <= slot + KEY_AHEAD < TILES:
+                key_stage(slot + KEY_AHEAD)
+            if slot >= 0:
+                value_bank = psum_v.tile([P, CHUNK], F32, tag="v", name="value_bank")
+                product(value_bank, weight_v, slot)
+            if 0 <= slot + FEATURE_AHEAD < TILES:
+                feature_stage(slot + FEATURE_AHEAD)
+            if slot >= 0:
+                weigh_stage(slot, value_bank)
 
         results = BATCH * H_TILES
         nc.vector.tensor_reduce(

@@ -31,6 +31,9 @@ KEY_AHEAD = 3
 QUANTISE_AHEAD = 5
 TRANSPOSE_AHEAD = 9
 SUM_BLOCK = 3
+LAST_CHUNK = CHUNKS - 1
+RESULTS = BATCH * H_TILES
+LATE_RESULTS = H_TILES
 
 FLOPS = 2 * BATCH * SEQ * D * (2 * H)
 
@@ -91,9 +94,17 @@ def tile_linearattention_pa_t_kernel(tc, x, Wk, bk, Wv, bv, out_0, out_1):
             nc.vector.tensor_copy(out=bias[:], in_=bias_bank[:, 0 : 2 * H_TILES])
             nc.vector.tensor_scalar_add(out=bk_plus_1[:], in0=bias[:, 0:H_TILES], scalar1=1.0)
             nc.vector.tensor_scalar_mul(out=minus_bk[:], in0=bias[:, 0:H_TILES], scalar1=-1.0)
+            for n in range(BATCH - 1):
+                nc.gpsimd.tensor_copy(
+                    out=value_bias[:, n * H_TILES : (n + 1) * H_TILES], in_=bias[:, H_TILES : 2 * H_TILES]
+                )
 
-        parts = const.tile([P, 2, 2 * BATCH * H_TILES * CHUNKS_PER_BATCH], F32)
-        nc.vector.memset(parts[:], 0.0)
+        parts = const.tile([P, 2, 2 * CHUNKS_PER_BATCH, RESULTS], F32)
+        nc.gpsimd.memset(parts[:], 0.0)
+        last_parts = [const.tile([P, P], F32, name="last_parts%d" % piece) for piece in range(2)]
+        for piece in range(2):
+            nc.gpsimd.memset(last_parts[piece][:], 0.0)
+        value_bias = const.tile([P, RESULTS - LATE_RESULTS], F32)
 
         def regroup_weight(raw, label):
             grouped = w_pool.tile([P, PASSES * H * PACK], BF16, name="grouped_" + label, align_bytes=64)
@@ -158,10 +169,14 @@ def tile_linearattention_pa_t_kernel(tc, x, Wk, bk, Wv, bv, out_0, out_1):
                     stop=(g == PASSES - 1),
                 )
 
-        def part_column(tile):
+        def part(plane, tile, piece=0):
             c, j = divmod(tile, H_TILES)
             n, chunk_of_batch = divmod(c, CHUNKS_PER_BATCH)
-            return 2 * ((n * H_TILES + j) * CHUNKS_PER_BATCH + chunk_of_batch)
+            result = n * H_TILES + j
+            if c == LAST_CHUNK:
+                column = plane * RESULTS + result
+                return last_parts[piece][:, column : column + 1]
+            return parts[:, plane, 2 * chunk_of_batch + piece, result : result + 1]
 
         key_banks = {}
         small_exps = {}
@@ -172,7 +187,6 @@ def tile_linearattention_pa_t_kernel(tc, x, Wk, bk, Wv, bv, out_0, out_1):
 
         def sum_feature(tile):
             j = tile % H_TILES
-            column = part_column(tile)
             depth = work.tile([P, CHUNK], F32, tag="depth", name="depth")
             nc.scalar.activation(
                 out=depth[:], in_=key_banks[tile][:], func=ACT.Relu, bias=minus_bk[:, j : j + 1], scale=-1.0
@@ -183,7 +197,7 @@ def tile_linearattention_pa_t_kernel(tc, x, Wk, bk, Wv, bv, out_0, out_1):
                 in_=key_banks[tile][:],
                 func=ACT.Relu,
                 bias=bias[:, j : j + 1],
-                accum_out=parts[:, 1, column : column + 1],
+                accum_out=part(1, tile),
             )
             decay = work.tile([P, CHUNK], F32, tag="decay", name="decay")
             nc.scalar.activation(
@@ -191,7 +205,7 @@ def tile_linearattention_pa_t_kernel(tc, x, Wk, bk, Wv, bv, out_0, out_1):
                 in_=depth[:],
                 func=ACT.Exp,
                 scale=-1.0,
-                accum_out=parts[:, 1, column + 1 : column + 2],
+                accum_out=part(1, tile, 1),
             )
             features[tile] = work.tile([P, CHUNK], F32, tag="feature", name="feature")
             nc.gpsimd.tensor_tensor(out=features[tile][:], in0=rise[:], in1=decay[:], op=ALU.add)
@@ -220,7 +234,6 @@ def tile_linearattention_pa_t_kernel(tc, x, Wk, bk, Wv, bv, out_0, out_1):
             if on_scalar(tile):
                 return
             j = tile % H_TILES
-            column = part_column(tile)
             features[tile] = work.tile([P, CHUNK], F32, tag="feature", name="feature")
             nc.vector.scalar_tensor_tensor(
                 out=features[tile][:],
@@ -229,22 +242,34 @@ def tile_linearattention_pa_t_kernel(tc, x, Wk, bk, Wv, bv, out_0, out_1):
                 in1=small_exps[tile][:],
                 op0=ALU.add,
                 op1=ALU.max,
-                accum_out=parts[:, 1, column : column + 1],
+                accum_out=part(1, tile),
             )
 
         def weigh_stage(tile, bank):
             j = tile % H_TILES
-            column = part_column(tile)
+            late = tile >= TILES - CHUNKS_PER_BATCH * H_TILES
             weighted = work.tile([P, CHUNK], F32, tag="weighted")
             nc.vector.scalar_tensor_tensor(
                 out=weighted[:],
                 in0=bank[:],
-                scalar=bias[:, H_TILES + j : H_TILES + j + 1],
+                scalar=bias[:, H_TILES + j : H_TILES + j + 1] if late else 0.0,
                 in1=features[tile][:],
                 op0=ALU.add,
                 op1=ALU.mult,
-                accum_out=parts[:, 0, column : column + 1],
+                accum_out=part(0, tile),
             )
+
+        def add_up():
+            halves = const.tile([P, 2, 2, RESULTS], F32)
+            nc.gpsimd.tensor_tensor(out=halves[:], in0=parts[:, :, 0:2, :], in1=parts[:, :, 2:4, :], op=ALU.add)
+            sums = totals[:, 0 : 2 * RESULTS].rearrange("p (w r) -> p w r", w=2)
+            nc.gpsimd.tensor_tensor(out=sums, in0=halves[:, :, 0, :], in1=halves[:, :, 1, :], op=ALU.add)
+            early = RESULTS - LATE_RESULTS
+            correction = const.tile([P, early], F32)
+            nc.gpsimd.tensor_tensor(
+                out=correction[:], in0=totals[:, RESULTS : RESULTS + early], in1=value_bias[:], op=ALU.mult
+            )
+            nc.gpsimd.tensor_tensor(out=totals[:, 0:early], in0=totals[:, 0:early], in1=correction[:], op=ALU.add)
 
         for unit in range(PASSES):
             transpose_unit(unit)
@@ -264,9 +289,14 @@ def tile_linearattention_pa_t_kernel(tc, x, Wk, bk, Wv, bv, out_0, out_1):
             unit, rest = divmod(slot + TRANSPOSE_AHEAD, UNIT_TILES)
             if rest == 0 and unit < UNITS:
                 transpose_unit(unit)
+            if slot == LAST_CHUNK * H_TILES:
+                add_up()
             if 0 <= slot + KEY_AHEAD < TILES:
                 key_stage(slot + KEY_AHEAD)
-            if slot >= 0:
+            if slot == TILES - 1:
+                value_bank = psum_t.tile([P, CHUNK], F32, tag="t", name="value_bank")
+                product(value_bank, weight_v, slot)
+            elif slot >= 0:
                 value_bank = psum_v.tile([P, CHUNK], F32, tag="v", name="value_bank")
                 product(value_bank, weight_v, slot)
             if 0 <= slot + FEATURE_AHEAD < TILES:
@@ -274,16 +304,18 @@ def tile_linearattention_pa_t_kernel(tc, x, Wk, bk, Wv, bv, out_0, out_1):
             if slot >= 0:
                 weigh_stage(slot, value_bank)
 
-        results = BATCH * H_TILES
-        nc.vector.tensor_reduce(
-            out=totals[:, 0 : 2 * results],
-            in_=parts[:].rearrange("p w (r k) -> p (w r) k", k=2 * CHUNKS_PER_BATCH),
-            axis=AXIS.X,
-            op=ALU.add,
-        )
-        totals_bank = psum_t.tile([P, P], F32, tag="t")
-        nc.tensor.transpose(totals_bank[:], totals[:], ident[:])
+        rows_bank = psum_t.tile([P, P], F32, tag="t", name="rows_bank")
+        pieces = [totals] + last_parts[::-1]
+        for i, piece in enumerate(pieces):
+            nc.tensor.matmul(
+                rows_bank[:],
+                lhsT=piece[:],
+                rhs=ident[:],
+                is_transpose=True,
+                start=(i == 0),
+                stop=(i == len(pieces) - 1),
+            )
         rows = const.tile([P, P], F32)
-        nc.vector.tensor_copy(out=rows[:], in_=totals_bank[:])
-        nc.sync.dma_start(out=out_0.rearrange("n (j h) -> (n j) h", h=P), in_=rows[0:results, :])
-        nc.sync.dma_start(out=out_1.rearrange("n (j h) -> (n j) h", h=P), in_=rows[results : 2 * results, :])
+        nc.scalar.copy(out=rows[:], in_=rows_bank[:])
+        nc.sync.dma_start(out=out_0.rearrange("n (j h) -> (n j) h", h=P), in_=rows[0:RESULTS, :])
+        nc.scalar.dma_start(out=out_1.rearrange("n (j h) -> (n j) h", h=P), in_=rows[RESULTS : 2 * RESULTS, :])

@@ -31,6 +31,8 @@ KEY_AHEAD = 3
 QUANTISE_AHEAD = 5
 TRANSPOSE_AHEAD = 9
 SUM_BLOCK = 3
+SUM_FROM = 2 * H_TILES
+WARM_UP_MATMULS = 4
 LAST_CHUNK = CHUNKS - 1
 RESULTS = BATCH * H_TILES
 LATE_RESULTS = H_TILES
@@ -54,25 +56,30 @@ def tile_linearattention_pa_t_kernel(tc, x, Wk, bk, Wv, bv, out_0, out_1):
         x_chunks = x.flatten_outer_dims().rearrange("(c p r) d -> c p (r d)", p=P, r=ROWS)
         x_tiles = [x_pool.tile([P, ROWS * D], BF16, name="x%d" % c) for c in range(CHUNKS)]
 
-        def load_weight(w, label):
-            raw = w_pool.tile([P, PASSES * PACK, H], BF16, name="raw_" + label)
-            for g in range(PASSES):
-                nc.sync.dma_start(
-                    out=raw[:, g * PACK : (g + 1) * PACK, :].rearrange("p t h -> p (t h)"),
-                    in_=w[g * P * PACK : (g + 1) * P * PACK, :].rearrange("(p t) h -> p (t h)", t=PACK),
-                )
-            return raw
+        raw_k = w_pool.tile([P, PASSES * PACK, H], BF16)
+        raw_v = w_pool.tile([P, PASSES * PACK, H], BF16)
+
+        def load_weight_pass(w, raw, g):
+            nc.sync.dma_start(
+                out=raw[:, g * PACK : (g + 1) * PACK, :].rearrange("p t h -> p (t h)"),
+                in_=w[g * P * PACK : (g + 1) * P * PACK, :].rearrange("(p t) h -> p (t h)", t=PACK),
+            )
+
+        def load_chunk(c):
+            nc.sync.dma_start(out=x_tiles[c][:], in_=x_chunks[c])
 
         bias_rows = const.tile([P, P], BF16)
         nc.vector.memset(bias_rows[:], 0.0)
-        nc.sync.dma_start(out=x_tiles[0][:], in_=x_chunks[0])
+        load_chunk(0)
         nc.sync.dma_start(out=bias_rows[0:H_TILES, :], in_=bk.rearrange("(j h) -> j h", h=P))
         nc.sync.dma_start(out=bias_rows[H_TILES : 2 * H_TILES, :], in_=bv.rearrange("(j h) -> j h", h=P))
-        raw_k = load_weight(Wk, "k")
-        nc.sync.dma_start(out=x_tiles[1][:], in_=x_chunks[1])
-        raw_v = load_weight(Wv, "v")
+        for g in range(PASSES):
+            load_weight_pass(Wk, raw_k, g)
+        load_weight_pass(Wv, raw_v, 0)
+        load_chunk(1)
+        load_weight_pass(Wv, raw_v, 1)
         for c in range(2, CHUNKS):
-            nc.sync.dma_start(out=x_tiles[c][:], in_=x_chunks[c])
+            load_chunk(c)
 
         ident = const.tile([P, P], F32)
         make_identity(nc, ident[:])
@@ -82,6 +89,8 @@ def tile_linearattention_pa_t_kernel(tc, x, Wk, bk, Wv, bv, out_0, out_1):
         nc.scalar.activation(out=warm[:, 1:2], in_=warm[:, 0:1], func=ACT.Exp)
         totals = const.tile([P, P], F32)
         nc.vector.memset(totals[:], 0.0)
+        zeros = const.tile([P, CHUNK], BF16)
+        nc.vector.memset(zeros[:], 0.0)
         bias_rows_f32 = const.tile([P, P], F32)
         nc.vector.tensor_copy(out=bias_rows_f32[:], in_=bias_rows[:])
         bias = const.tile([P, 2 * H_TILES], F32)
@@ -106,16 +115,14 @@ def tile_linearattention_pa_t_kernel(tc, x, Wk, bk, Wv, bv, out_0, out_1):
             nc.gpsimd.memset(last_parts[piece][:], 0.0)
         value_bias = const.tile([P, RESULTS - LATE_RESULTS], F32)
 
-        def regroup_weight(raw, label):
-            grouped = w_pool.tile([P, PASSES * H * PACK], BF16, name="grouped_" + label, align_bytes=64)
-            for g in range(PASSES):
-                nc.vector.tensor_copy(
-                    out=grouped[:, g * H * PACK : (g + 1) * H * PACK].rearrange(
-                        "p (c i t) -> p c t i", i=4, t=PACK
-                    ),
-                    in_=raw[:, g * PACK : (g + 1) * PACK, :].rearrange("p t (c i) -> p c t i", i=4),
-                )
-            return grouped
+        grouped_k = w_pool.tile([P, PASSES * H * PACK], BF16, align_bytes=64)
+        grouped_v = w_pool.tile([P, PASSES * H * PACK], BF16, align_bytes=64)
+
+        def regroup_pass(raw, grouped, g, copy):
+            copy(
+                out=grouped[:, g * H * PACK : (g + 1) * H * PACK].rearrange("p (c i t) -> p c t i", i=4, t=PACK),
+                in_=raw[:, g * PACK : (g + 1) * PACK, :].rearrange("p t (c i) -> p c t i", i=4),
+            )
 
         def quantise_weight(grouped, label):
             codes = w_pool.tile([P, PASSES * H], U32, name="codes_" + label, align_bytes=64)
@@ -183,7 +190,7 @@ def tile_linearattention_pa_t_kernel(tc, x, Wk, bk, Wv, bv, out_0, out_1):
         features = {}
 
         def on_scalar(tile):
-            return tile % H_TILES == SUM_BLOCK and tile >= H_TILES
+            return tile % H_TILES == SUM_BLOCK and tile >= SUM_FROM
 
         def sum_feature(tile):
             j = tile % H_TILES
@@ -271,18 +278,27 @@ def tile_linearattention_pa_t_kernel(tc, x, Wk, bk, Wv, bv, out_0, out_1):
             )
             nc.gpsimd.tensor_tensor(out=totals[:, 0:early], in0=totals[:, 0:early], in1=correction[:], op=ALU.add)
 
-        for unit in range(PASSES):
-            transpose_unit(unit)
-        grouped_k = regroup_weight(raw_k, "k")
-        spread_biases()
-        weight_k = quantise_weight(grouped_k, "k")
-        quantise_chunk(0)
-        grouped_v = regroup_weight(raw_v, "v")
-        weight_v = None
+        def warm_up():
+            unread = psum_v.tile([P, CHUNK], F32, tag="v", name="unread")
+            for i in range(WARM_UP_MATMULS):
+                nc.tensor.matmul(unread[:], lhsT=zeros[:, 0:P], rhs=zeros[:], start=True, stop=True)
 
-        for slot in range(-5, TILES):
-            if slot == -2:
-                weight_v = quantise_weight(grouped_v, "v")
+        transpose_unit(0)
+        transpose_unit(1)
+        for g in range(PASSES):
+            regroup_pass(raw_k, grouped_k, g, nc.vector.tensor_copy)
+        spread_biases()
+        warm_up()
+        weight_k = quantise_weight(grouped_k, "k")
+        regroup_pass(raw_v, grouped_v, 0, nc.scalar.copy)
+        quantise_chunk(0)
+        transpose_unit(2)
+        key_stage(0)
+        transpose_unit(3)
+        regroup_pass(raw_v, grouped_v, 1, nc.vector.tensor_copy)
+        weight_v = quantise_weight(grouped_v, "v")
+
+        for slot in range(1 - KEY_AHEAD, TILES):
             chunk, rest = divmod(slot + QUANTISE_AHEAD, H_TILES)
             if rest == 0 and 0 < chunk < CHUNKS:
                 quantise_chunk(chunk)
@@ -291,7 +307,7 @@ def tile_linearattention_pa_t_kernel(tc, x, Wk, bk, Wv, bv, out_0, out_1):
                 transpose_unit(unit)
             if slot == LAST_CHUNK * H_TILES:
                 add_up()
-            if 0 <= slot + KEY_AHEAD < TILES:
+            if slot + KEY_AHEAD < TILES:
                 key_stage(slot + KEY_AHEAD)
             if slot == TILES - 1:
                 value_bank = psum_t.tile([P, CHUNK], F32, tag="t", name="value_bank")

@@ -33,6 +33,7 @@ TRANSPOSE_AHEAD = 9
 SUM_BLOCK = 3
 SUM_FROM = 2 * H_TILES
 WARM_UP_MATMULS = 4
+OPERAND_ALIGN = 256
 LAST_CHUNK = CHUNKS - 1
 RESULTS = BATCH * H_TILES
 LATE_RESULTS = H_TILES
@@ -115,8 +116,8 @@ def tile_linearattention_pa_t_kernel(tc, x, Wk, bk, Wv, bv, out_0, out_1):
             nc.gpsimd.memset(last_parts[piece][:], 0.0)
         value_bias = const.tile([P, RESULTS - LATE_RESULTS], F32)
 
-        grouped_k = w_pool.tile([P, PASSES * H * PACK], BF16, align_bytes=64)
-        grouped_v = w_pool.tile([P, PASSES * H * PACK], BF16, align_bytes=64)
+        grouped_k = w_pool.tile([P, PASSES * H * PACK], BF16, align_bytes=OPERAND_ALIGN)
+        grouped_v = w_pool.tile([P, PASSES * H * PACK], BF16, align_bytes=OPERAND_ALIGN)
 
         def regroup_pass(raw, grouped, g, copy):
             copy(
@@ -125,8 +126,8 @@ def tile_linearattention_pa_t_kernel(tc, x, Wk, bk, Wv, bv, out_0, out_1):
             )
 
         def quantise_weight(grouped, label):
-            codes = w_pool.tile([P, PASSES * H], U32, name="codes_" + label, align_bytes=64)
-            scales = w_pool.tile([P, PASSES * H], U8, name="scales_" + label, align_bytes=64)
+            codes = w_pool.tile([P, PASSES * H], U32, name="codes_" + label, align_bytes=OPERAND_ALIGN)
+            scales = w_pool.tile([P, PASSES * H], U8, name="scales_" + label, align_bytes=OPERAND_ALIGN)
             nc.vector.quantize_mx(out=codes[:].bitcast(FP8X4), scales=scales[:], in_=grouped[:])
             return codes, scales
 
@@ -136,7 +137,7 @@ def tile_linearattention_pa_t_kernel(tc, x, Wk, bk, Wv, bv, out_0, out_1):
         def transpose_unit(unit):
             c, g = divmod(unit, PASSES)
             if g == 0:
-                grouped_x[c] = xq_pool.tile([P, PASSES * CHUNK * PACK], BF16, name="grouped_x", align_bytes=64)
+                grouped_x[c] = xq_pool.tile([P, PASSES * CHUNK * PACK], BF16, name="grouped_x", align_bytes=OPERAND_ALIGN)
             words_in = x_tiles[c][:].bitcast(F32)
             words_out = grouped_x[c][:].bitcast(F32)
             for half in range(2):
@@ -154,8 +155,8 @@ def tile_linearattention_pa_t_kernel(tc, x, Wk, bk, Wv, bv, out_0, out_1):
                 )
 
         def quantise_chunk(c):
-            codes = xq_pool.tile([P, PASSES * CHUNK], U32, name="codes_x", align_bytes=64)
-            scales = xq_pool.tile([P, PASSES * CHUNK], U8, name="scales_x", align_bytes=64)
+            codes = xq_pool.tile([P, PASSES * CHUNK], U32, name="codes_x", align_bytes=OPERAND_ALIGN)
+            scales = xq_pool.tile([P, PASSES * CHUNK], U8, name="scales_x", align_bytes=OPERAND_ALIGN)
             nc.vector.quantize_mx(out=codes[:].bitcast(FP8X4), scales=scales[:], in_=grouped_x[c][:])
             x_codes[c] = (codes, scales)
 

@@ -28,10 +28,10 @@ UNIT_TILES = H_TILES // PASSES
 
 FEATURE_AHEAD = 1
 KEY_AHEAD = 3
-QUANTISE_AHEAD = 5
+QUANTISE_AHEAD = 6
 TRANSPOSE_AHEAD = 9
 SUM_BLOCK = 3
-SUM_FROM = 2 * H_TILES
+SUM_FROM = 4 * H_TILES
 WARM_UP_MATMULS = 4
 OPERAND_ALIGN = 256
 LAST_CHUNK = CHUNKS - 1
@@ -98,23 +98,18 @@ def tile_linearattention_pa_t_kernel(tc, x, Wk, bk, Wv, bv, out_0, out_1):
         bk_plus_1 = const.tile([P, H_TILES], F32)
         minus_bk = const.tile([P, H_TILES], F32)
 
+        bias_bank = psum_v.tile([P, P], F32, tag="v", name="bias_bank")
+
         def spread_biases():
-            bias_bank = psum_t.tile([P, P], F32, tag="t")
-            nc.tensor.transpose(bias_bank[:], bias_rows_f32[:], ident[:])
             nc.vector.tensor_copy(out=bias[:], in_=bias_bank[:, 0 : 2 * H_TILES])
             nc.vector.tensor_scalar_add(out=bk_plus_1[:], in0=bias[:, 0:H_TILES], scalar1=1.0)
             nc.vector.tensor_scalar_mul(out=minus_bk[:], in0=bias[:, 0:H_TILES], scalar1=-1.0)
-            for n in range(BATCH - 1):
-                nc.gpsimd.tensor_copy(
-                    out=value_bias[:, n * H_TILES : (n + 1) * H_TILES], in_=bias[:, H_TILES : 2 * H_TILES]
-                )
 
         parts = const.tile([P, 2, 2 * CHUNKS_PER_BATCH, RESULTS], F32)
         nc.gpsimd.memset(parts[:], 0.0)
         last_parts = [const.tile([P, P], F32, name="last_parts%d" % piece) for piece in range(2)]
         for piece in range(2):
             nc.gpsimd.memset(last_parts[piece][:], 0.0)
-        value_bias = const.tile([P, RESULTS - LATE_RESULTS], F32)
 
         grouped_k = w_pool.tile([P, PASSES * H * PACK], BF16, align_bytes=OPERAND_ALIGN)
         grouped_v = w_pool.tile([P, PASSES * H * PACK], BF16, align_bytes=OPERAND_ALIGN)
@@ -275,7 +270,10 @@ def tile_linearattention_pa_t_kernel(tc, x, Wk, bk, Wv, bv, out_0, out_1):
             early = RESULTS - LATE_RESULTS
             correction = const.tile([P, early], F32)
             nc.gpsimd.tensor_tensor(
-                out=correction[:], in0=totals[:, RESULTS : RESULTS + early], in1=value_bias[:], op=ALU.mult
+                out=correction[:].rearrange("p (n j) -> p n j", j=H_TILES),
+                in0=totals[:, RESULTS : RESULTS + early].rearrange("p (n j) -> p n j", j=H_TILES),
+                in1=bias[:, H_TILES : 2 * H_TILES].unsqueeze(1).to_broadcast([P, BATCH - 1, H_TILES]),
+                op=ALU.mult,
             )
             nc.gpsimd.tensor_tensor(out=totals[:, 0:early], in0=totals[:, 0:early], in1=correction[:], op=ALU.add)
 
@@ -288,11 +286,12 @@ def tile_linearattention_pa_t_kernel(tc, x, Wk, bk, Wv, bv, out_0, out_1):
         transpose_unit(1)
         for g in range(PASSES):
             regroup_pass(raw_k, grouped_k, g, nc.vector.tensor_copy)
-        spread_biases()
+        nc.tensor.transpose(bias_bank[:], bias_rows_f32[:], ident[:])
         warm_up()
         weight_k = quantise_weight(grouped_k, "k")
         regroup_pass(raw_v, grouped_v, 0, nc.scalar.copy)
         quantise_chunk(0)
+        spread_biases()
         transpose_unit(2)
         key_stage(0)
         transpose_unit(3)
@@ -300,9 +299,6 @@ def tile_linearattention_pa_t_kernel(tc, x, Wk, bk, Wv, bv, out_0, out_1):
         weight_v = quantise_weight(grouped_v, "v")
 
         for slot in range(1 - KEY_AHEAD, TILES):
-            chunk, rest = divmod(slot + QUANTISE_AHEAD, H_TILES)
-            if rest == 0 and 0 < chunk < CHUNKS:
-                quantise_chunk(chunk)
             unit, rest = divmod(slot + TRANSPOSE_AHEAD, UNIT_TILES)
             if rest == 0 and unit < UNITS:
                 transpose_unit(unit)
@@ -318,6 +314,9 @@ def tile_linearattention_pa_t_kernel(tc, x, Wk, bk, Wv, bv, out_0, out_1):
                 product(value_bank, weight_v, slot)
             if 0 <= slot + FEATURE_AHEAD < TILES:
                 feature_stage(slot + FEATURE_AHEAD)
+            chunk, rest = divmod(slot + QUANTISE_AHEAD, H_TILES)
+            if rest == 0 and chunk < CHUNKS:
+                quantise_chunk(chunk)
             if slot >= 0:
                 weigh_stage(slot, value_bank)
 

from contextlib import ExitStack

import concourse.mybir as mybir
from concourse.masks import make_identity

F32 = mybir.dt.float32
BF16 = mybir.dt.bfloat16
U32 = mybir.dt.uint32
U8 = mybir.dt.uint8
FP8X4 = mybir.dt.float8_e4m3fn_x4
ACT = mybir.ActivationFunctionType
ALU = mybir.AluOpType
AXIS = mybir.AxisListType

P = 128
PACK = 4
BATCH, SEQ, D, H = 4, 1024, 1024, 512
PASSES = D // (P * PACK)
CHUNK = 512
CHUNKS = BATCH * SEQ // CHUNK
CHUNKS_PER_BATCH = SEQ // CHUNK
ROWS = CHUNK // P
WORDS = D // 2
H_TILES = H // P
UNITS = CHUNKS * PASSES
TILES = CHUNKS * H_TILES
UNIT_TILES = H_TILES // PASSES

FEATURE_AHEAD = 1
KEY_AHEAD = 3
QUANTISE_AHEAD = 6
TRANSPOSE_AHEAD = 9
SUM_BLOCK = 3
SUM_FROM = 4 * H_TILES
WARM_UP_MATMULS = 4
OPERAND_ALIGN = 256
LAST_CHUNK = CHUNKS - 1
RESULTS = BATCH * H_TILES
LATE_RESULTS = H_TILES

FLOPS = 2 * BATCH * SEQ * D * (2 * H)


def tile_linearattention_pa_t_kernel(tc, x, Wk, bk, Wv, bv, out_0, out_1):
    nc = tc.nc
    with ExitStack() as ctx:
        ctx.enter_context(tc.manual_schedule())
        const = ctx.enter_context(tc.tile_pool(name="const", bufs=1))
        x_pool = ctx.enter_context(tc.tile_pool(name="x", bufs=1))
        w_pool = ctx.enter_context(tc.tile_pool(name="w", bufs=1))
        xq_pool = ctx.enter_context(tc.tile_pool(name="xq", bufs=3))
        work = ctx.enter_context(tc.tile_pool(name="work", bufs=4))
        psum_t = ctx.enter_context(tc.psum_pool(name="psum_t", bufs=2))
        psum_k = ctx.enter_context(tc.psum_pool(name="psum_k", bufs=4))
        psum_v = ctx.enter_context(tc.psum_pool(name="psum_v", bufs=2))

        x_chunks = x.flatten_outer_dims().rearrange("(c p r) d -> c p (r d)", p=P, r=ROWS)
        x_tiles = [x_pool.tile([P, ROWS * D], BF16, name="x%d" % c) for c in range(CHUNKS)]

        raw_k = w_pool.tile([P, PASSES * PACK, H], BF16)
        raw_v = w_pool.tile([P, PASSES * PACK, H], BF16)

        def load_weight_pass(w, raw, g):
            nc.sync.dma_start(
                out=raw[:, g * PACK : (g + 1) * PACK, :].rearrange("p t h -> p (t h)"),
                in_=w[g * P * PACK : (g + 1) * P * PACK, :].rearrange("(p t) h -> p (t h)", t=PACK),
            )

        def load_chunk(c):
            nc.sync.dma_start(out=x_tiles[c][:], in_=x_chunks[c])

        bias_rows = const.tile([P, P], BF16)
        nc.vector.memset(bias_rows[:], 0.0)
        load_chunk(0)
        nc.sync.dma_start(out=bias_rows[0:H_TILES, :], in_=bk.rearrange("(j h) -> j h", h=P))
        nc.sync.dma_start(out=bias_rows[H_TILES : 2 * H_TILES, :], in_=bv.rearrange("(j h) -> j h", h=P))
        for g in range(PASSES):
            load_weight_pass(Wk, raw_k, g)
        load_weight_pass(Wv, raw_v, 0)
        load_chunk(1)
        load_weight_pass(Wv, raw_v, 1)
        for c in range(2, CHUNKS):
            load_chunk(c)

        ident = const.tile([P, P], F32)
        make_identity(nc, ident[:])

        warm = const.tile([P, 2], F32)
        nc.vector.memset(warm[:], 0.0)
        nc.scalar.activation(out=warm[:, 1:2], in_=warm[:, 0:1], func=ACT.Exp)
        totals = const.tile([P, P], F32)
        nc.vector.memset(totals[:], 0.0)
        zeros = const.tile([P, CHUNK], BF16)
        nc.vector.memset(zeros[:], 0.0)
        bias_rows_f32 = const.tile([P, P], F32)
        nc.vector.tensor_copy(out=bias_rows_f32[:], in_=bias_rows[:])
        bias = const.tile([P, 2 * H_TILES], F32)
        bk_plus_1 = const.tile([P, H_TILES], F32)
        minus_bk = const.tile([P, H_TILES], F32)

        bias_bank = psum_v.tile([P, P], F32, tag="v", name="bias_bank")

        def spread_biases():
            nc.vector.tensor_copy(out=bias[:], in_=bias_bank[:, 0 : 2 * H_TILES])
            nc.vector.tensor_scalar_add(out=bk_plus_1[:], in0=bias[:, 0:H_TILES], scalar1=1.0)
            nc.vector.tensor_scalar_mul(out=minus_bk[:], in0=bias[:, 0:H_TILES], scalar1=-1.0)

        parts = const.tile([P, 2, 2 * CHUNKS_PER_BATCH, RESULTS], F32)
        nc.gpsimd.memset(parts[:], 0.0)
        last_parts = [const.tile([P, P], F32, name="last_parts%d" % piece) for piece in range(2)]
        for piece in range(2):
            nc.gpsimd.memset(last_parts[piece][:], 0.0)

        grouped_k = w_pool.tile([P, PASSES * H * PACK], BF16, align_bytes=OPERAND_ALIGN)
        grouped_v = w_pool.tile([P, PASSES * H * PACK], BF16, align_bytes=OPERAND_ALIGN)

        def regroup_pass(raw, grouped, g, copy):
            copy(
                out=grouped[:, g * H * PACK : (g + 1) * H * PACK].rearrange("p (c i t) -> p c t i", i=4, t=PACK),
                in_=raw[:, g * PACK : (g + 1) * PACK, :].rearrange("p t (c i) -> p c t i", i=4),
            )

        def quantise_weight(grouped, label):
            codes = w_pool.tile([P, PASSES * H], U32, name="codes_" + label, align_bytes=OPERAND_ALIGN)
            scales = w_pool.tile([P, PASSES * H], U8, name="scales_" + label, align_bytes=OPERAND_ALIGN)
            nc.vector.quantize_mx(out=codes[:].bitcast(FP8X4), scales=scales[:], in_=grouped[:])
            return codes, scales

        grouped_x = {}
        x_codes = {}

        def transpose_unit(unit):
            c, g = divmod(unit, PASSES)
            if g == 0:
                grouped_x[c] = xq_pool.tile([P, PASSES * CHUNK * PACK], BF16, name="grouped_x", align_bytes=OPERAND_ALIGN)
            words_in = x_tiles[c][:].bitcast(F32)
            words_out = grouped_x[c][:].bitcast(F32)
            for half in range(2):
                bank = psum_t.tile([P, 2, 2 * P], F32, tag="t")
                for u in range(2):
                    for r in range(2):
                        row = (2 * half + r) * WORDS + 2 * P * g
                        nc.tensor.transpose(
                            bank[:, u, r * P : (r + 1) * P], words_in[:, row + u : row + 2 * P : 2], ident[:]
                        )
                start = 2 * (g * CHUNK + half * 2 * P)
                nc.scalar.copy(
                    out=words_out[:, start : start + 4 * P].rearrange("p (s u) -> p s u", u=2),
                    in_=bank[:].rearrange("p u s -> p s u"),
                )

        def quantise_chunk(c):
            codes = xq_pool.tile([P, PASSES * CHUNK], U32, name="codes_x", align_bytes=OPERAND_ALIGN)
            scales = xq_pool.tile([P, PASSES * CHUNK], U8, name="scales_x", align_bytes=OPERAND_ALIGN)
            nc.vector.quantize_mx(out=codes[:].bitcast(FP8X4), scales=scales[:], in_=grouped_x[c][:])
            x_codes[c] = (codes, scales)

        def product(bank, weight, tile):
            c, j = divmod(tile, H_TILES)
            w_codes, w_scales = weight
            codes, scales = x_codes[c]
            for g in range(PASSES):
                w_cols = slice(g * H + j * P, g * H + (j + 1) * P)
                x_cols = slice(g * CHUNK, (g + 1) * CHUNK)
                nc.tensor.matmul_mx(
                    out=bank[:],
                    lhsT=w_codes[:, w_cols].bitcast(FP8X4),
                    lhsT_scale=w_scales[:, w_cols],
                    rhs=codes[:, x_cols].bitcast(FP8X4),
                    rhs_scale=scales[:, x_cols],
                    start=(g == 0),
                    stop=(g == PASSES - 1),
                )

        def part(plane, tile, piece=0):
            c, j = divmod(tile, H_TILES)
            n, chunk_of_batch = divmod(c, CHUNKS_PER_BATCH)
            result = n * H_TILES + j
            if c == LAST_CHUNK:
                column = plane * RESULTS + result
                return last_parts[piece][:, column : column + 1]
            return parts[:, plane, 2 * chunk_of_batch + piece, result : result + 1]

        key_banks = {}
        small_exps = {}
        features = {}

        def on_scalar(tile):
            return tile % H_TILES == SUM_BLOCK and tile >= SUM_FROM

        def sum_feature(tile):
            j = tile % H_TILES
            depth = work.tile([P, CHUNK], F32, tag="depth", name="depth")
            nc.scalar.activation(
                out=depth[:], in_=key_banks[tile][:], func=ACT.Relu, bias=minus_bk[:, j : j + 1], scale=-1.0
            )
            rise = work.tile([P, CHUNK], F32, tag="rise", name="rise")
            nc.scalar.activation(
                out=rise[:],
                in_=key_banks[tile][:],
                func=ACT.Relu,
                bias=bias[:, j : j + 1],
                accum_out=part(1, tile),
            )
            decay = work.tile([P, CHUNK], F32, tag="decay", name="decay")
            nc.scalar.activation(
                out=decay[:],
                in_=depth[:],
                func=ACT.Exp,
                scale=-1.0,
                accum_out=part(1, tile, 1),
            )
            features[tile] = work.tile([P, CHUNK], F32, tag="feature", name="feature")
            nc.gpsimd.tensor_tensor(out=features[tile][:], in0=rise[:], in1=decay[:], op=ALU.add)

        def key_stage(tile):
            j = tile % H_TILES
            key_banks[tile] = psum_k.tile([P, CHUNK], F32, tag="k", name="key_bank")
            product(key_banks[tile], weight_k, tile)
            if on_scalar(tile):
                sum_feature(tile)
                return
            small_exps[tile] = work.tile([P, CHUNK], F32, tag="small_exp", name="small_exp")
            nc.scalar.activation(
                out=small_exps[tile][:], in_=key_banks[tile][:], func=ACT.Exp, bias=bias[:, j : j + 1]
            )
            nc.gpsimd.tensor_scalar(
                out=small_exps[tile][:],
                in0=small_exps[tile][:],
                scalar1=1.0,
                scalar2=0.0,
                op0=ALU.min,
                op1=ALU.max,
            )

        def feature_stage(tile):
            if on_scalar(tile):
                return
            j = tile % H_TILES
            features[tile] = work.tile([P, CHUNK], F32, tag="feature", name="feature")
            nc.vector.scalar_tensor_tensor(
                out=features[tile][:],
                in0=key_banks[tile][:],
                scalar=bk_plus_1[:, j : j + 1],
                in1=small_exps[tile][:],
                op0=ALU.add,
                op1=ALU.max,
                accum_out=part(1, tile),
            )

        def weigh_stage(tile, bank):
            j = tile % H_TILES
            late = tile >= TILES - CHUNKS_PER_BATCH * H_TILES
            weighted = work.tile([P, CHUNK], F32, tag="weighted")
            nc.vector.scalar_tensor_tensor(
                out=weighted[:],
                in0=bank[:],
                scalar=bias[:, H_TILES + j : H_TILES + j + 1] if late else 0.0,
                in1=features[tile][:],
                op0=ALU.add,
                op1=ALU.mult,
                accum_out=part(0, tile),
            )

        def add_up():
            halves = const.tile([P, 2, 2, RESULTS], F32)
            nc.gpsimd.tensor_tensor(out=halves[:], in0=parts[:, :, 0:2, :], in1=parts[:, :, 2:4, :], op=ALU.add)
            sums = totals[:, 0 : 2 * RESULTS].rearrange("p (w r) -> p w r", w=2)
            nc.gpsimd.tensor_tensor(out=sums, in0=halves[:, :, 0, :], in1=halves[:, :, 1, :], op=ALU.add)
            early = RESULTS - LATE_RESULTS
            correction = const.tile([P, early], F32)
            nc.gpsimd.tensor_tensor(
                out=correction[:].rearrange("p (n j) -> p n j", j=H_TILES),
                in0=totals[:, RESULTS : RESULTS + early].rearrange("p (n j) -> p n j", j=H_TILES),
                in1=bias[:, H_TILES : 2 * H_TILES].unsqueeze(1).to_broadcast([P, BATCH - 1, H_TILES]),
                op=ALU.mult,
            )
            nc.gpsimd.tensor_tensor(out=totals[:, 0:early], in0=totals[:, 0:early], in1=correction[:], op=ALU.add)

        def warm_up():
            unread = psum_v.tile([P, CHUNK], F32, tag="v", name="unread")
            for i in range(WARM_UP_MATMULS):
                nc.tensor.matmul(unread[:], lhsT=zeros[:, 0:P], rhs=zeros[:], start=True, stop=True)

        transpose_unit(0)
        transpose_unit(1)
        for g in range(PASSES):
            regroup_pass(raw_k, grouped_k, g, nc.vector.tensor_copy)
        nc.tensor.transpose(bias_bank[:], bias_rows_f32[:], ident[:])
        warm_up()
        weight_k = quantise_weight(grouped_k, "k")
        regroup_pass(raw_v, grouped_v, 0, nc.scalar.copy)
        quantise_chunk(0)
        spread_biases()
        transpose_unit(2)
        key_stage(0)
        transpose_unit(3)
        regroup_pass(raw_v, grouped_v, 1, nc.vector.tensor_copy)
        weight_v = quantise_weight(grouped_v, "v")

        for slot in range(1 - KEY_AHEAD, TILES):
            unit, rest = divmod(slot + TRANSPOSE_AHEAD, UNIT_TILES)
            if rest == 0 and unit < UNITS:
                transpose_unit(unit)
            if slot == LAST_CHUNK * H_TILES:
                add_up()
            if slot + KEY_AHEAD < TILES:
                key_stage(slot + KEY_AHEAD)
            if slot == TILES - 1:
                value_bank = psum_t.tile([P, CHUNK], F32, tag="t", name="value_bank")
                product(value_bank, weight_v, slot)
            elif slot >= 0:
                value_bank = psum_v.tile([P, CHUNK], F32, tag="v", name="value_bank")
                product(value_bank, weight_v, slot)
            if 0 <= slot + FEATURE_AHEAD < TILES:
                feature_stage(slot + FEATURE_AHEAD)
            chunk, rest = divmod(slot + QUANTISE_AHEAD, H_TILES)
            if rest == 0 and chunk < CHUNKS:
                quantise_chunk(chunk)
            if slot >= 0:
                weigh_stage(slot, value_bank)

        rows_bank = psum_t.tile([P, P], F32, tag="t", name="rows_bank")
        pieces = [totals] + last_parts[::-1]
        for i, piece in enumerate(pieces):
            nc.tensor.matmul(
                rows_bank[:],
                lhsT=piece[:],
                rhs=ident[:],
                is_transpose=True,
                start=(i == 0),
                stop=(i == len(pieces) - 1),
            )
        rows = const.tile([P, P], F32)
        nc.scalar.copy(out=rows[:], in_=rows_bank[:])
        nc.sync.dma_start(out=out_0.rearrange("n (j h) -> (n j) h", h=P), in_=rows[0:RESULTS, :])
        nc.scalar.dma_start(out=out_1.rearrange("n (j h) -> (n j) h", h=P), in_=rows[RESULTS : 2 * RESULTS, :])
